import numpy as np
import ml_dtypes


def mxq(x, axis, fmt="e4m3"):
    dtype, down = {"e4m3": (ml_dtypes.float8_e4m3fn, 7), "e5m2": (ml_dtypes.float8_e5m2, 14)}[fmt]
    v = np.moveaxis(np.asarray(x, np.float32).astype(ml_dtypes.bfloat16).astype(np.float64), axis, -1)
    blocks = v.reshape(v.shape[:-1] + (-1, 32))
    amax = np.abs(blocks).max(-1, keepdims=True)
    byte = np.maximum(np.where(amax > 0, np.frexp(amax)[1] - 1 + 127, 0) - down, 1)
    scale = np.exp2(byte - 127.0)
    codes = (blocks / scale).astype(np.float32).astype(dtype).astype(np.float64)
    return np.moveaxis((codes * scale).reshape(v.shape), -1, axis)


WIDE = False


def mx_kscale(k):
    if not WIDE:
        return np.ones(k)
    levels = np.array([18, -18])
    if k % 512:
        return np.exp2(np.random.permutation(np.resize(levels, k // 32))).repeat(32)
    a = np.empty((k // 512, 16))
    for p in range(k // 512):
        a[p, :8] = np.random.permutation(np.resize(levels, 8))
        for g in range(8):
            far = levels[np.abs(levels - a[p, g]) >= 10]
            a[p, g + 8] = far[np.random.randint(len(far))]
    return np.exp2(a.ravel()).repeat(32)


BF16 = ml_dtypes.bfloat16


def bf(x):
    return np.asarray(x, np.float32).astype(BF16)


def f64(x):
    return np.asarray(x).astype(np.float64)


N, D, H, HD = 1024, 768, 16, 64
P = H * HD
HALF = HD // 2
EPS = 1e-6


def rotate_half(z):
    h = z.shape[-1] // 2
    return np.concatenate([-z[..., h:], z[..., :h]], axis=-1)


def rope_grad(g, cos, sin):
    def ap(z, c, s):
        return z * c[:, None, :] - rotate_half(z * s[:, None, :])

    return np.concatenate([ap(g[..., :HALF], cos[:, :HALF], sin[:, :HALF]), ap(g[..., HALF:], cos[:, HALF:], sin[:, HALF:])], axis=-1)


def norm_grad(y, dn):
    r = 1.0 / np.sqrt(np.mean(y * y, axis=-1, keepdims=True) + EPS)
    return r * (dn - y * (r * r) * np.mean(dn * y, axis=-1, keepdims=True))


def per_head(f):
    h = np.arange(H)
    return np.repeat(f[h * HD + 32 * (h % 2)], HD)


def setup_inputs():
    s = mx_kscale(N)
    uq = per_head(mx_kscale(P))
    uk = per_head(mx_kscale(P))
    uv = per_head(mx_kscale(P))
    x0 = bf(np.random.standard_normal((N, D)))
    cos = bf(np.random.uniform(-1.0, 1.0, (N, HD)))
    sin = bf(np.random.uniform(-1.0, 1.0, (N, HD)))
    wq0 = bf(np.random.standard_normal((D, P)) / np.sqrt(D))
    wk0 = bf(np.random.standard_normal((D, P)) / np.sqrt(D))
    wv0 = bf(np.random.standard_normal((D, P)) / np.sqrt(D))
    q_scale = bf(1.0 + 0.1 * np.random.standard_normal(HD))
    k_scale = bf(1.0 + 0.1 * np.random.standard_normal(HD))
    yq = f64(x0) @ f64(wq0)
    yk = f64(x0) @ f64(wk0)
    yv = f64(x0) @ f64(wv0)

    def grad(u):
        g = np.random.standard_normal((N, H, HD)) * np.exp2(np.random.randint(-6, 1, (N, 1, 1)))
        return bf(g / s[:, None, None] * u.reshape(1, H, HD))

    g0 = grad(uq)
    g1 = grad(uk)
    g2 = grad(uv)
    return {
        "hidden_states": bf(f64(x0) * s[:, None]),
        "cos": cos,
        "sin": sin,
        "Wq": bf(f64(wq0) / uq),
        "Wk": bf(f64(wk0) / uk),
        "Wv": bf(f64(wv0) / uv),
        "q_scale": q_scale,
        "k_scale": k_scale,
        "yq": np.asarray(yq, np.float32),
        "yk": np.asarray(yk, np.float32),
        "yv": np.asarray(yv, np.float32),
        "grad_0": g0,
        "grad_1": g1,
        "grad_2": g2,
    }


def reference(hidden_states, cos, sin, Wq, Wk, Wv, q_scale, k_scale, yq, yk, yv, grad_0, grad_1, grad_2):
    c, s = f64(cos), f64(sin)
    dnq = rope_grad(f64(grad_0), c, s) * f64(q_scale)
    dnk = rope_grad(f64(grad_1), c, s) * f64(k_scale)
    dnv = f64(grad_2)
    dyq = norm_grad(f64(yq).reshape(N, H, HD), dnq).reshape(N, P)
    dyk = norm_grad(f64(yk).reshape(N, H, HD), dnk).reshape(N, P)
    dyv = norm_grad(f64(yv).reshape(N, H, HD), dnv).reshape(N, P)
    dy = np.concatenate([dyq, dyk, dyv], axis=1)
    w = np.concatenate([f64(Wq), f64(Wk), f64(Wv)], axis=1)
    dx = mxq(dy, 1, "e5m2") @ mxq(w, 1, "e4m3").T
    xt = mxq(f64(hidden_states), 0, "e4m3").T
    dwq = xt @ mxq(dyq, 0, "e5m2")
    dwk = xt @ mxq(dyk, 0, "e5m2")
    dwv = xt @ mxq(dyv, 0, "e5m2")
    return dx, dwq, dwk, dwv

@@ -1,0 +1,482 @@
+from contextlib import ExitStack
+
+import concourse.mybir as mybir
+from concourse.masks import make_identity
+
+N, D, H, HD = 1024, 768, 16, 64
+P = H * HD
+PARTS = 128
+PACK = 4
+PASS = PARTS * PACK
+EPS = 1e-6
+FLOPS = 2 * 2 * N * D * 3 * P
+
+F32 = mybir.dt.float32
+BF16 = mybir.dt.bfloat16
+U32 = mybir.dt.uint32
+U8 = mybir.dt.uint8
+E4 = mybir.dt.float8_e4m3fn_x4
+E5 = mybir.dt.float8_e5m2_x4
+
+ALU = mybir.AluOpType
+ACT = mybir.ActivationFunctionType
+AX = mybir.AxisListType
+
+UNITS = 12
+HEADS = 8
+GROUPS = PACK * HEADS
+FBLK = 16
+D_TILES = D // PARTS
+
+
+def tile_torchgemma4visionattention_pa_v_kernel(
+    tc, hidden_states, cos, sin, Wq, Wk, Wv, q_scale, k_scale, yq, yk, yv, grad_0, grad_1, grad_2, out_0, out_1, out_2, out_3
+):
+    nc = tc.nc
+    ys = (yq, yk, yv)
+    grads = (grad_0, grad_1, grad_2)
+    ws = (Wq, Wk, Wv)
+    dws = (out_1, out_2, out_3)
+
+    def proj_of(i):
+        return i % 3
+
+    def half_of(i):
+        return (i // 3) % 2
+
+    def g_of(i):
+        return i // 6
+
+    with ExitStack() as ctx:
+        const = ctx.enter_context(tc.tile_pool(name="const", bufs=1))
+        io = ctx.enter_context(tc.tile_pool(name="io", bufs=3))
+        work = ctx.enter_context(tc.tile_pool(name="work", bufs=2))
+        stat = ctx.enter_context(tc.tile_pool(name="stat", bufs=3))
+        keep = ctx.enter_context(tc.tile_pool(name="keep", bufs=8))
+        stage = ctx.enter_context(tc.tile_pool(name="stage", bufs=4))
+        ps_red = ctx.enter_context(tc.psum_pool(name="ps_red", bufs=1))
+        ps_tp = ctx.enter_context(tc.psum_pool(name="ps_tp", bufs=3))
+        ps_mx = ctx.enter_context(tc.psum_pool(name="ps_mx", bufs=4))
+        ctx.enter_context(tc.manual_schedule())
+
+        ident = const.tile([PARTS, PARTS], F32)
+        make_identity(nc, ident[:])
+        junk = const.tile([PARTS, GROUPS * HD], BF16)
+        w_codes = const.tile([PARTS, 6, D], U32, align_bytes=64)
+        w_scales = const.tile([PARTS, 6, D], U8, align_bytes=64)
+        x_codes = const.tile([PARTS, 2, D], U32, align_bytes=64)
+        x_scales = const.tile([PARTS, 2, D], U8, align_bytes=64)
+
+        st = [dict() for i in range(UNITS)]
+        raws = dict()
+
+        def load_unit(i):
+            rows = slice(g_of(i) * PASS, (g_of(i) + 1) * PASS)
+            cols = slice(half_of(i) * PASS, (half_of(i) + 1) * PASS)
+            y = io.tile([PARTS, PACK, PASS], F32)
+            nc.sync.dma_start(out=y[:], in_=ys[proj_of(i)][rows, cols].rearrange("(p j) w -> p j w", j=PACK))
+            g = io.tile([PARTS, PACK, PASS], BF16)
+            gsrc = grads[proj_of(i)].rearrange("n h f -> n (h f)")
+            nc.sync.dma_start(out=g[:], in_=gsrc[rows, cols].rearrange("(p j) w -> p j w", j=PACK))
+            st[i]["y"] = y
+            st[i]["g"] = g
+
+        def load_w(c):
+            raw = work.tile([PARTS, D_TILES, PASS], BF16, tag="raw", name="w_raw", align_bytes=64)
+            cols = slice(half_of(c) * PASS, (half_of(c) + 1) * PASS)
+            nc.sync.dma_start(out=raw[:], in_=ws[proj_of(c)][:, cols].rearrange("(t p) w -> p t w", p=PARTS))
+            raws["w", c] = raw
+
+        def load_x(g):
+            raw = work.tile([PARTS, PACK, D], BF16, tag="raw", name="x_raw", align_bytes=64)
+            nc.sync.dma_start(out=raw[:], in_=hidden_states[g * PASS : (g + 1) * PASS, :].rearrange("(p j) w -> p j w", j=PACK))
+            raws["x", g] = raw
+
+        c_raw = const.tile([PARTS, 2, PACK, HD], BF16)
+        s_raw = const.tile([PARTS, 2, PACK, HD], BF16)
+        qs = const.tile([PARTS, HD], BF16)
+        ks = const.tile([PARTS, HD], BF16)
+        load_unit(0)
+        nc.sync.dma_start(out=c_raw[:], in_=cos.rearrange("(g p j) f -> p g j f", g=2, j=PACK))
+        nc.sync.dma_start(out=s_raw[:], in_=sin.rearrange("(g p j) f -> p g j f", g=2, j=PACK))
+        nc.sync.dma_start(out=qs[:], in_=q_scale.partition_broadcast(PARTS))
+        nc.sync.dma_start(out=ks[:], in_=k_scale.partition_broadcast(PARTS))
+        load_unit(1)
+        load_x(0)
+        load_w(0)
+
+        tabs = []
+        for scale, tname in ((qs, "tab_q"), (ks, "tab_k")):
+            tab = const.tile([PARTS, 2 * PACK, 2, HD], F32, name=tname)
+            nc.vector.tensor_tensor(
+                out=tab[:, :, 0, :],
+                in0=c_raw[:].rearrange("p g j f -> p (g j) f"),
+                in1=scale[:].unsqueeze(1).to_broadcast([PARTS, 2 * PACK, HD]),
+                op=ALU.mult,
+            )
+            t6 = tab[:].rearrange("p t s (b k i) -> p t s b k i", b=2, k=2)
+            s5 = s_raw[:].rearrange("p g j (b k i) -> p (g j) b k i", b=2, k=2)
+            q4 = scale[:].rearrange("p (b k i) -> p b k i", b=2, k=2)
+            for k in range(2):
+                for b in range(2):
+                    nc.vector.tensor_tensor(
+                        out=t6[:, :, 1, b, k, :],
+                        in0=s5[:, :, b, k, :],
+                        in1=q4[:, b, 1 - k, :].unsqueeze(1).to_broadcast([PARTS, 2 * PACK, 16]),
+                        op=ALU.mult,
+                    )
+            tabs.append(tab)
+
+        def squares(i, lo, hi):
+            if lo == 0:
+                ss = stat.tile([PARTS, GROUPS], F32)
+                st[i]["ss"] = ss
+            y = st[i]["y"]
+            for q in range(lo, hi):
+                j, h = q // HEADS, q % HEADS
+                nc.scalar.activation(
+                    out=junk[:, q * HD : (q + 1) * HD],
+                    in_=y[:, j, h * HD : (h + 1) * HD],
+                    func=ACT.Square,
+                    accum_out=st[i]["ss"][:, q : q + 1],
+                )
+
+        def norms(i):
+            r = stat.tile([PARTS, GROUPS], F32)
+            nc.scalar.activation(out=r[:], in_=st[i]["ss"][:], func=ACT.Abs_reciprocal_sqrt, scale=1.0 / HD, bias=EPS)
+            rr = stat.tile([PARTS, GROUPS], F32)
+            nc.scalar.activation(out=rr[:], in_=r[:], func=ACT.Square)
+            st[i]["r"] = r
+            st[i]["rr"] = rr
+
+        def new_pair(i):
+            pair = work.tile([PARTS, GROUPS, 2, HD], F32)
+            st[i]["pair"] = pair
+
+        def scale_v(i, lo, hi):
+            if lo == 0:
+                gr = io.tile([PARTS, GROUPS, HD], F32, tag="gr", name="gr", bufs=1)
+                st[i]["gr"] = gr
+            for q in range(lo, hi):
+                j, h = q // HEADS, q % HEADS
+                nc.scalar.activation(
+                    out=st[i]["gr"][:, q, :],
+                    in_=st[i]["g"][:, j, h * HD : (h + 1) * HD],
+                    func=ACT.Copy,
+                    scale=st[i]["r"][:, q : q + 1],
+                )
+
+        def rope_products(i):
+            new_pair(i)
+            tab = tabs[proj_of(i)]
+            for q in range(GROUPS):
+                j, h = q // HEADS, q % HEADS
+                nc.vector.scalar_tensor_tensor(
+                    out=st[i]["pair"][:, q, :, :],
+                    in0=st[i]["g"][:, j, h * HD : (h + 1) * HD].unsqueeze(1).to_broadcast([PARTS, 2, HD]),
+                    scalar=st[i]["r"][:, q : q + 1],
+                    in1=tab[:, g_of(i) * PACK + j, :, :],
+                    op0=ALU.mult,
+                    op1=ALU.mult,
+                )
+
+        def rope_add(i, k):
+            v = st[i]["pair"][:].rearrange("p q s (b k i) -> p q s b k i", b=2, k=2)
+            nc.vector.tensor_tensor(
+                out=v[:, :, 0, :, k, :],
+                in0=v[:, :, 0, :, k, :],
+                in1=v[:, :, 1, :, 1 - k, :],
+                op=ALU.add if k == 0 else ALU.subtract,
+            )
+
+        def products(i):
+            if proj_of(i) == 2:
+                new_pair(i)
+            pair = st[i]["pair"]
+            nc.vector.tensor_tensor(
+                out=pair[:, :, 1, :],
+                in0=st[i]["gr"][:] if proj_of(i) == 2 else pair[:, :, 0, :],
+                in1=st[i]["y"][:].rearrange("p j (h f) -> p (j h) f", f=HD),
+                op=ALU.mult,
+            )
+
+        def fold(i):
+            red = ps_red.tile([PARTS, GROUPS, FBLK], F32)
+            for b in range(HD // FBLK):
+                nc.tensor.matmul(
+                    out=red[:],
+                    lhsT=ident[:],
+                    rhs=st[i]["pair"][:, :, 1, b * FBLK : (b + 1) * FBLK],
+                    start=(b == 0),
+                    stop=(b == HD // FBLK - 1),
+                )
+            st[i]["red"] = red
+
+        def dots(i):
+            dot = stat.tile([PARTS, GROUPS], F32)
+            nc.vector.tensor_reduce(out=dot[:], in_=st[i]["red"][:], axis=AX.X, op=ALU.add)
+            st[i]["dot"] = dot
+
+        def coefs(i):
+            nb = stat.tile([PARTS, GROUPS], F32)
+            nc.vector.scalar_tensor_tensor(
+                out=nb[:], in0=st[i]["dot"][:], scalar=-1.0 / HD, in1=st[i]["rr"][:], op0=ALU.mult, op1=ALU.mult
+            )
+            st[i]["nb"] = nb
+
+        def finish(i):
+            dy = work.tile([PARTS, PACK, PASS], BF16)
+            for q in range(GROUPS):
+                j, h = q // HEADS, q % HEADS
+                cols = slice(h * HD, (h + 1) * HD)
+                nc.vector.scalar_tensor_tensor(
+                    out=dy[:, j, cols],
+                    in0=st[i]["y"][:, j, cols],
+                    scalar=st[i]["nb"][:, q : q + 1],
+                    in1=st[i]["gr"][:, q, :] if proj_of(i) == 2 else st[i]["pair"][:, q, 0, :],
+                    op0=ALU.mult,
+                    op1=ALU.add,
+                )
+            st[i]["dy"] = dy
+
+        def transposes(i):
+            words = st[i]["dy"][:].rearrange("p j c -> p (j c)").bitcast(F32)
+            half_words = PASS // 2
+            st[i]["tp"] = []
+            for b in range(2):
+                bank = ps_tp.tile([PARTS, 2, 2, PARTS], F32, tag="tp", name="tp")
+                for jj in range(2):
+                    j = 2 * b + jj
+                    for u in range(2):
+                        nc.tensor.transpose(bank[:, jj, u, :], words[:, j * half_words + u : (j + 1) * half_words : 2], ident[:])
+                st[i]["tp"].append(bank)
+
+        def copy_t(i, b):
+            if b == 0:
+                dyt = work.tile([PARTS, PASS, PACK], BF16, align_bytes=64)
+                st[i]["dyt"] = dyt
+            words = st[i]["dyt"][:].rearrange("p n t -> p (n t)").bitcast(F32)
+            dst = words[:, b * PASS : (b + 1) * PASS].rearrange("p (j n u) -> p j n u", j=2, u=2)
+            nc.scalar.copy(out=dst, in_=st[i]["tp"][b][:].rearrange("p j u n -> p j n u"))
+
+        def interleave(i):
+            dyi = work.tile([PARTS, PASS, PACK], BF16, align_bytes=64)
+            nc.scalar.copy(out=dyi[:], in_=st[i]["dy"][:].rearrange("p j c -> p c j"))
+            st[i]["dyi"] = dyi
+
+        def quant_f(i):
+            fc = keep.tile([PARTS, PASS], U32, align_bytes=64)
+            fs = keep.tile([PARTS, PASS], U8, align_bytes=64)
+            nc.vector.quantize_mx(out=fc[:].bitcast(E5), scales=fs[:], in_=st[i]["dyt"][:].rearrange("p n t -> p (n t)"))
+            st[i]["f"] = (fc, fs)
+
+        def quant_t(i):
+            tcod = keep.tile([PARTS, PASS], U32, align_bytes=64)
+            tsc = keep.tile([PARTS, PASS], U8, align_bytes=64)
+            nc.vector.quantize_mx(out=tcod[:].bitcast(E5), scales=tsc[:], in_=st[i]["dyi"][:].rearrange("p c j -> p (c j)"))
+            st[i]["t"] = (tcod, tsc)
+
+        def quant_768(src, codes, scales):
+            flat = src[:].rearrange("p n t -> p (n t)")
+            for lo, hi in ((0, 512), (512, 768)):
+                nc.vector.quantize_mx(
+                    out=codes[:, lo:hi].bitcast(E4), scales=scales[:, lo:hi], in_=flat[:, lo * PACK : hi * PACK]
+                )
+
+        def w_transposes(c):
+            raws["wt", c] = []
+            words = raws["w", c][:].rearrange("p t w -> p (t w)").bitcast(F32)
+            half_words = PASS // 2
+            for b in range(3):
+                bank = ps_tp.tile([PARTS, 2, 2, PARTS], F32, tag="tp", name="tp")
+                for tt in range(2):
+                    t = 2 * b + tt
+                    for u in range(2):
+                        nc.tensor.transpose(bank[:, tt, u, :], words[:, t * half_words + u : (t + 1) * half_words : 2], ident[:])
+                raws["wt", c].append(bank)
+
+        def w_copy(c, b):
+            if b == 0:
+                grp = work.tile([PARTS, D, PACK], BF16, tag="grp", name="w_grp", align_bytes=64)
+                raws["wg", c] = grp
+            words = raws["wg", c][:].rearrange("p n t -> p (n t)").bitcast(F32)
+            dst = words[:, b * PASS : (b + 1) * PASS].rearrange("p (j n u) -> p j n u", j=2, u=2)
+            nc.scalar.copy(out=dst, in_=raws["wt", c][b][:].rearrange("p j u n -> p j n u"))
+
+        def w_quant(c):
+            quant_768(raws["wg", c], w_codes[:, c, :], w_scales[:, c, :])
+
+        def x_inter(g):
+            grp = work.tile([PARTS, D, PACK], BF16, tag="grp", name="x_grp", align_bytes=64)
+            nc.vector.tensor_copy(out=grp[:], in_=raws["x", g][:].rearrange("p j w -> p w j"))
+            raws["xg", g] = grp
+
+        def x_quant(g):
+            quant_768(raws["xg", g], x_codes[:, g, :], x_scales[:, g, :])
+
+        def copy_out(engine, out, in_):
+            if engine == "s":
+                nc.scalar.copy(out=out, in_=in_)
+            else:
+                nc.vector.tensor_copy(out=out, in_=in_)
+
+        def dw_task(i, t, engine):
+            acc = ps_mx.tile([PARTS, PASS], F32, tag="mx", name="acc")
+            for g in range(2):
+                src = i - 6 + 6 * g
+                tcod, tsc = st[src]["t"]
+                lanes = slice(t * PARTS, (t + 1) * PARTS)
+                nc.tensor.matmul_mx(
+                    out=acc[:],
+                    lhsT=x_codes[:, g, lanes].bitcast(E4),
+                    lhsT_scale=x_scales[:, g, lanes],
+                    rhs=tcod[:].bitcast(E5),
+                    rhs_scale=tsc[:],
+                    start=(g == 0),
+                    stop=(g == 1),
+                )
+
+            def empty():
+                res = stage.tile([PARTS, PASS], F32, tag="dw", name="res")
+                copy_out(engine, res[:], acc[:])
+                cols = slice(half_of(i) * PASS, (half_of(i) + 1) * PASS)
+                nc.sync.dma_start(out=dws[proj_of(i)][t * PARTS : (t + 1) * PARTS, cols], in_=res[:])
+
+            return [empty]
+
+        def dx_task(g, j, units, engine, mode):
+            banks = []
+            for d0 in (0, D - PASS):
+                acc = ps_mx.tile([PARTS, PASS], F32, tag="mx", name="acc")
+                banks.append(acc)
+            lanes = slice(j * PARTS, (j + 1) * PARTS)
+            for n, i in enumerate(units):
+                fc, fs = st[i]["f"]
+                for acc, d0 in zip(banks, (0, D - PASS)):
+                    nc.tensor.matmul_mx(
+                        out=acc[:],
+                        lhsT=fc[:, lanes].bitcast(E5),
+                        lhsT_scale=fs[:, lanes],
+                        rhs=w_codes[:, i % 6, d0 : d0 + PASS].bitcast(E4),
+                        rhs_scale=w_scales[:, i % 6, d0 : d0 + PASS],
+                        start=(n == 0),
+                        stop=(n == len(units) - 1),
+                    )
+            rest = D - PASS
+
+            def store(res):
+                dst = out_0[g * PASS : (g + 1) * PASS, :].rearrange("(p j) d -> p j d", j=PACK)
+                nc.sync.dma_start(out=dst[:, j, :], in_=res)
+
+            def empty():
+                if mode == "part":
+                    if j % 2 == 0:
+                        part = work.tile([PARTS, 2, D], F32, tag="raw", name="part", align_bytes=64)
+                        raws["part", j // 2] = part
+                    res = raws["part", j // 2][:, j % 2, :]
+                else:
+                    full = stage.tile([PARTS, D], F32, tag="dx", name="full", bufs=2)
+                    res = full[:]
+                pieces = ((slice(0, PASS), banks[0][:]), (slice(PASS, D), banks[1][:, PASS - rest :]))
+                for cols, src in pieces:
+                    if mode == "add":
+                        nc.vector.tensor_tensor(out=res[:, cols], in0=src, in1=raws["part", j // 2][:, j % 2, cols], op=ALU.add)
+                    else:
+                        copy_out(engine, res[:, cols], src)
+                if mode != "part":
+                    store(res)
+
+            return [empty]
+
+        mx = dict()
+        mx[8] = [lambda j=j: dx_task(0, j, range(6), "s", "full") for j in (0, 1)]
+        mx[9] = [lambda: dx_task(0, 2, range(6), "s", "full")] + [lambda t=t: dw_task(6, t, "s") for t in range(D_TILES)]
+        mx[10] = [lambda: dx_task(0, 3, range(6), "s", "full")] + [lambda t=t: dw_task(7, t, "s") for t in range(D_TILES)]
+        mx[11] = [lambda t=t: dw_task(8, t, "s") for t in range(D_TILES)] + [
+            lambda j=j: dx_task(1, j, range(6, 9), "s", "part") for j in (0, 1)
+        ]
+        mx[12] = [lambda t=t: dw_task(9, t, "s") for t in range(D_TILES)] + [
+            lambda j=j: dx_task(1, j, range(6, 9), "s", "part") for j in (2, 3)
+        ]
+        mx[13] = [lambda t=t: dw_task(10, t, "s") for t in range(D_TILES)]
+        mx[14] = [lambda j=j: dx_task(1, j, range(9, 12), "v", "add") for j in range(4)] + [
+            lambda t=t: dw_task(11, t, "s") for t in range(D_TILES)
+        ]
+
+        def s_items(k):
+            items = []
+            if 0 <= k - 2 < UNITS:
+                items.append(lambda: interleave(k - 2))
+                items.append(lambda: copy_t(k - 2, 0))
+                items.append(lambda: copy_t(k - 2, 1))
+            if 1 <= k <= 6:
+                for b in range(3):
+                    items.append(lambda b=b: w_copy(k - 1, b))
+            if k + 1 < UNITS:
+                for lo in range(0, GROUPS, 8):
+                    items.append(lambda lo=lo: squares(k + 1, lo, lo + 8))
+                items.append(lambda: norms(k + 1))
+                if proj_of(k + 1) == 2:
+                    for lo in range(0, GROUPS, 16):
+                        items.append(lambda lo=lo: scale_v(k + 1, lo, lo + 16))
+            return items
+
+        def v_step(k):
+            rope = k < UNITS and proj_of(k) < 2
+            prev = 0 <= k - 1 < UNITS
+            quant = 0 <= k - 2 < UNITS
+            if rope:
+                rope_products(k)
+                if quant:
+                    quant_f(k - 2)
+                rope_add(k, 0)
+            if prev:
+                dots(k - 1)
+            if 2 <= k <= 7:
+                w_quant(k - 2)
+            if rope:
+                rope_add(k, 1)
+            if prev:
+                coefs(k - 1)
+            if k < UNITS:
+                products(k)
+            if k in (0, 7):
+                x_inter(k // 7)
+            if prev:
+                finish(k - 1)
+            if quant and not rope:
+                quant_f(k - 2)
+            if quant:
+                quant_t(k - 2)
+            if k in (0, 7):
+                x_quant(k // 7)
+
+        squares(0, 0, GROUPS)
+        norms(0)
+        for k in range(UNITS + 3):
+            if 0 <= k - 1 < UNITS:
+                fold(k - 1)
+            if 0 <= k - 2 < UNITS:
+                transposes(k - 2)
+            if 1 <= k <= 6:
+                w_transposes(k - 1)
+            items = s_items(k)
+            tasks = mx.get(k, [])
+            waiting = []
+            for n in range(max(len(items), len(tasks))):
+                if n < len(items):
+                    items[n]()
+                for copy in waiting:
+                    copy()
+                waiting = []
+                if n < len(tasks):
+                    waiting = tasks[n]()
+            for copy in waiting:
+                copy()
+            v_step(k)
+            if k + 2 < UNITS:
+                load_unit(k + 2)
+            if k + 1 < 6:
+                load_w(k + 1)
+            if k == 5:
+                load_x(1)

@@ -25,7 +25,8 @@ AX = mybir.AxisListType
 UNITS = 12
 HEADS = 8
 GROUPS = PACK * HEADS
-FBLK = 16
+FOLDS = 16
+QUAD = 4
 D_TILES = D // PARTS
 
 
@@ -54,14 +55,14 @@ def tile_torchgemma4visionattention_pa_v_kernel(
         stat = ctx.enter_context(tc.tile_pool(name="stat", bufs=3))
         keep = ctx.enter_context(tc.tile_pool(name="keep", bufs=8))
         stage = ctx.enter_context(tc.tile_pool(name="stage", bufs=4))
-        ps_red = ctx.enter_context(tc.psum_pool(name="ps_red", bufs=1))
-        ps_tp = ctx.enter_context(tc.psum_pool(name="ps_tp", bufs=3))
+        ps_red = ctx.enter_context(tc.psum_pool(name="ps_red", bufs=2))
+        ps_tp = ctx.enter_context(tc.psum_pool(name="ps_tp", bufs=2))
         ps_mx = ctx.enter_context(tc.psum_pool(name="ps_mx", bufs=4))
-        ctx.enter_context(tc.manual_schedule())
 
         ident = const.tile([PARTS, PARTS], F32)
         make_identity(nc, ident[:])
-        junk = const.tile([PARTS, GROUPS * HD], BF16)
+        picks = const.tile([PARTS, GROUPS], F32)
+        nc.vector.tensor_reduce(out=picks[:], in_=ident[:].rearrange("p (g q) -> p g q", q=QUAD), axis=AX.X, op=ALU.add)
         w_codes = const.tile([PARTS, 6, D], U32, align_bytes=64)
         w_scales = const.tile([PARTS, 6, D], U8, align_bytes=64)
         x_codes = const.tile([PARTS, 2, D], U32, align_bytes=64)
@@ -73,7 +74,7 @@ def tile_torchgemma4visionattention_pa_v_kernel(
         def load_unit(i):
             rows = slice(g_of(i) * PASS, (g_of(i) + 1) * PASS)
             cols = slice(half_of(i) * PASS, (half_of(i) + 1) * PASS)
-            y = io.tile([PARTS, PACK, PASS], F32)
+            y = io.tile([PARTS, PACK, PASS], F32, bufs=4)
             nc.sync.dma_start(out=y[:], in_=ys[proj_of(i)][rows, cols].rearrange("(p j) w -> p j w", j=PACK))
             g = io.tile([PARTS, PACK, PASS], BF16)
             gsrc = grads[proj_of(i)].rearrange("n h f -> n (h f)")
@@ -103,6 +104,7 @@ def tile_torchgemma4visionattention_pa_v_kernel(
         nc.sync.dma_start(out=ks[:], in_=k_scale.partition_broadcast(PARTS))
         load_unit(1)
         load_x(0)
+        load_unit(2)
         load_w(0)
 
         tabs = []
@@ -127,117 +129,129 @@ def tile_torchgemma4visionattention_pa_v_kernel(
                     )
             tabs.append(tab)
 
-        def squares(i, lo, hi):
-            if lo == 0:
-                ss = stat.tile([PARTS, GROUPS], F32)
-                st[i]["ss"] = ss
-            y = st[i]["y"]
-            for q in range(lo, hi):
-                j, h = q // HEADS, q % HEADS
-                nc.scalar.activation(
-                    out=junk[:, q * HD : (q + 1) * HD],
-                    in_=y[:, j, h * HD : (h + 1) * HD],
-                    func=ACT.Square,
-                    accum_out=st[i]["ss"][:, q : q + 1],
+        def folded(tile):
+            return tile[:].rearrange("p (b g q) -> p g b q", b=FOLDS, q=QUAD)
+
+        def squares(i):
+            gr = io.tile([PARTS, GROUPS * HD], F32, tag="gr", name="gr")
+            st[i]["gr"] = gr
+            nc.scalar.activation(
+                out=folded(gr),
+                in_=st[i]["y"][:].rearrange("p j (h b q) -> p (j h) b q", b=FOLDS, q=QUAD),
+                func=ACT.Square,
+            )
+
+        def fold(src):
+            acc = ps_red.tile([PARTS, PASS], F32, tag="red", name="red")
+            for b in range(FOLDS):
+                nc.tensor.matmul(
+                    out=acc[:, 0:PARTS],
+                    lhsT=src[:, b * PARTS : (b + 1) * PARTS],
+                    rhs=ident[:],
+                    start=(b == 0),
+                    stop=(b == FOLDS - 1),
+                    is_transpose=True,
                 )
+            return acc
+
+        def fold_copy(acc):
+            part = stat.tile([PARTS, PARTS], F32, tag="fold", name="part_sum")
+            nc.scalar.copy(out=part[:], in_=acc[:, 0:PARTS])
+            return part
+
+        def fold_sum(acc, part):
+            res = acc[:, PARTS : PARTS + GROUPS]
+            nc.tensor.matmul(out=res, lhsT=part[:], rhs=picks[:], start=True, stop=True)
+            return res
 
         def norms(i):
             r = stat.tile([PARTS, GROUPS], F32)
-            nc.scalar.activation(out=r[:], in_=st[i]["ss"][:], func=ACT.Abs_reciprocal_sqrt, scale=1.0 / HD, bias=EPS)
+            nc.scalar.activation(out=r[:], in_=st[i]["ss"], func=ACT.Abs_reciprocal_sqrt, scale=1.0 / HD, bias=EPS)
             rr = stat.tile([PARTS, GROUPS], F32)
             nc.scalar.activation(out=rr[:], in_=r[:], func=ACT.Square)
             st[i]["r"] = r
             st[i]["rr"] = rr
 
-        def new_pair(i):
-            pair = work.tile([PARTS, GROUPS, 2, HD], F32)
-            st[i]["pair"] = pair
-
-        def scale_v(i, lo, hi):
-            if lo == 0:
-                gr = io.tile([PARTS, GROUPS, HD], F32, tag="gr", name="gr", bufs=1)
-                st[i]["gr"] = gr
+        def scale_g(i, lo, hi):
             for q in range(lo, hi):
-                j, h = q // HEADS, q % HEADS
+                cols = slice(q * HD, (q + 1) * HD)
                 nc.scalar.activation(
-                    out=st[i]["gr"][:, q, :],
-                    in_=st[i]["g"][:, j, h * HD : (h + 1) * HD],
+                    out=st[i]["gr"][:, cols],
+                    in_=st[i]["g"][:].rearrange("p j c -> p (j c)")[:, cols],
                     func=ACT.Copy,
                     scale=st[i]["r"][:, q : q + 1],
                 )
 
         def rope_products(i):
-            new_pair(i)
+            dn = work.tile([PARTS, GROUPS * HD], F32, tag="dn", name="dn")
+            gs = work.tile([PARTS, GROUPS * HD], F32, tag="gs", name="gs", bufs=1)
+            st[i]["dn"] = dn
+            st[i]["gs"] = gs
             tab = tabs[proj_of(i)]
-            for q in range(GROUPS):
-                j, h = q // HEADS, q % HEADS
-                nc.vector.scalar_tensor_tensor(
-                    out=st[i]["pair"][:, q, :, :],
-                    in0=st[i]["g"][:, j, h * HD : (h + 1) * HD].unsqueeze(1).to_broadcast([PARTS, 2, HD]),
-                    scalar=st[i]["r"][:, q : q + 1],
-                    in1=tab[:, g_of(i) * PACK + j, :, :],
-                    op0=ALU.mult,
-                    op1=ALU.mult,
+            src = st[i]["g"][:].rearrange("p j c -> p (j c)") if i == 0 else st[i]["gr"][:]
+            shape = [PARTS, PACK, HEADS, HD]
+            slots = slice(g_of(i) * PACK, (g_of(i) + 1) * PACK)
+            for n, dst in ((0, dn), (1, gs)):
+                nc.vector.tensor_tensor(
+                    out=dst[:].rearrange("p (j h f) -> p j h f", j=PACK, f=HD),
+                    in0=src.rearrange("p (j h f) -> p j h f", j=PACK, f=HD),
+                    in1=tab[:, slots, n, :].unsqueeze(2).to_broadcast(shape),
+                    op=ALU.mult,
                 )
 
         def rope_add(i, k):
-            v = st[i]["pair"][:].rearrange("p q s (b k i) -> p q s b k i", b=2, k=2)
+            dn = st[i]["dn"][:].rearrange("p (q k i) -> p q k i", k=2, i=16)
+            gs = st[i]["gs"][:].rearrange("p (q k i) -> p q k i", k=2, i=16)
             nc.vector.tensor_tensor(
-                out=v[:, :, 0, :, k, :],
-                in0=v[:, :, 0, :, k, :],
-                in1=v[:, :, 1, :, 1 - k, :],
-                op=ALU.add if k == 0 else ALU.subtract,
+                out=dn[:, :, k, :], in0=dn[:, :, k, :], in1=gs[:, :, 1 - k, :], op=ALU.add if k == 0 else ALU.subtract
             )
 
         def products(i):
             if proj_of(i) == 2:
-                new_pair(i)
-            pair = st[i]["pair"]
+                dst = work.tile([PARTS, GROUPS * HD], F32, tag="dn", name="prod_v")
+                src = st[i]["gr"]
+            else:
+                dst, src = st[i]["gr"], st[i]["dn"]
             nc.vector.tensor_tensor(
-                out=pair[:, :, 1, :],
-                in0=st[i]["gr"][:] if proj_of(i) == 2 else pair[:, :, 0, :],
-                in1=st[i]["y"][:].rearrange("p j (h f) -> p (j h) f", f=HD),
+                out=folded(dst),
+                in0=src[:].rearrange("p (g b q) -> p g b q", b=FOLDS, q=QUAD),
+                in1=st[i]["y"][:].rearrange("p j (h b q) -> p (j h) b q", b=FOLDS, q=QUAD),
                 op=ALU.mult,
             )
-
-        def fold(i):
-            red = ps_red.tile([PARTS, GROUPS, FBLK], F32)
-            for b in range(HD // FBLK):
-                nc.tensor.matmul(
-                    out=red[:],
-                    lhsT=ident[:],
-                    rhs=st[i]["pair"][:, :, 1, b * FBLK : (b + 1) * FBLK],
-                    start=(b == 0),
-                    stop=(b == HD // FBLK - 1),
-                )
-            st[i]["red"] = red
-
-        def dots(i):
-            dot = stat.tile([PARTS, GROUPS], F32)
-            nc.vector.tensor_reduce(out=dot[:], in_=st[i]["red"][:], axis=AX.X, op=ALU.add)
-            st[i]["dot"] = dot
+            st[i]["prod"] = dst
 
         def coefs(i):
             nb = stat.tile([PARTS, GROUPS], F32)
             nc.vector.scalar_tensor_tensor(
-                out=nb[:], in0=st[i]["dot"][:], scalar=-1.0 / HD, in1=st[i]["rr"][:], op0=ALU.mult, op1=ALU.mult
+                out=nb[:], in0=st[i]["dot"], scalar=-1.0 / HD, in1=st[i]["rr"][:], op0=ALU.mult, op1=ALU.mult
             )
             st[i]["nb"] = nb
 
         def finish(i):
             dy = work.tile([PARTS, PACK, PASS], BF16)
+            base = st[i]["gr"] if proj_of(i) == 2 else st[i]["dn"]
             for q in range(GROUPS):
                 j, h = q // HEADS, q % HEADS
                 cols = slice(h * HD, (h + 1) * HD)
                 nc.vector.scalar_tensor_tensor(
-                    out=dy[:, j, cols],
+                    out=st[i]["gr"][:, q * HD : (q + 1) * HD] if i == 0 else dy[:, j, cols],
                     in0=st[i]["y"][:, j, cols],
                     scalar=st[i]["nb"][:, q : q + 1],
-                    in1=st[i]["gr"][:, q, :] if proj_of(i) == 2 else st[i]["pair"][:, q, 0, :],
+                    in1=base[:, q * HD : (q + 1) * HD],
                     op0=ALU.mult,
                     op1=ALU.add,
                 )
             st[i]["dy"] = dy
+
+        def rescale(i):
+            for q in range(GROUPS):
+                j, h = q // HEADS, q % HEADS
+                nc.scalar.activation(
+                    out=st[i]["dy"][:, j, h * HD : (h + 1) * HD],
+                    in_=st[i]["gr"][:, q * HD : (q + 1) * HD],
+                    func=ACT.Copy,
+                    scale=st[i]["r"][:, q : q + 1],
+                )
 
         def transposes(i):
             words = st[i]["dy"][:].rearrange("p j c -> p (j c)").bitcast(F32)
@@ -261,7 +275,10 @@ def tile_torchgemma4visionattention_pa_v_kernel(
 
         def interleave(i):
             dyi = work.tile([PARTS, PASS, PACK], BF16, align_bytes=64)
-            nc.scalar.copy(out=dyi[:], in_=st[i]["dy"][:].rearrange("p j c -> p c j"))
+            nc.scalar.copy(
+                out=dyi[:].rearrange("p (c i) j -> p c j i", i=4),
+                in_=st[i]["dy"][:].rearrange("p j (c i) -> p c j i", i=4),
+            )
             st[i]["dyi"] = dyi
 
         def quant_f(i):
@@ -297,7 +314,7 @@ def tile_torchgemma4visionattention_pa_v_kernel(
 
         def w_copy(c, b):
             if b == 0:
-                grp = work.tile([PARTS, D, PACK], BF16, tag="grp", name="w_grp", align_bytes=64)
+                grp = work.tile([PARTS, D, PACK], BF16, tag="grp", name="w_grp", align_bytes=64, bufs=1)
                 raws["wg", c] = grp
             words = raws["wg", c][:].rearrange("p n t -> p (n t)").bitcast(F32)
             dst = words[:, b * PASS : (b + 1) * PASS].rearrange("p (j n u) -> p j n u", j=2, u=2)
@@ -307,7 +324,7 @@ def tile_torchgemma4visionattention_pa_v_kernel(
             quant_768(raws["wg", c], w_codes[:, c, :], w_scales[:, c, :])
 
         def x_inter(g):
-            grp = work.tile([PARTS, D, PACK], BF16, tag="grp", name="x_grp", align_bytes=64)
+            grp = work.tile([PARTS, D, PACK], BF16, tag="grp", name="x_grp", align_bytes=64, bufs=1)
             nc.vector.tensor_copy(out=grp[:], in_=raws["x", g][:].rearrange("p j w -> p w j"))
             raws["xg", g] = grp
 
@@ -406,19 +423,16 @@ def tile_torchgemma4visionattention_pa_v_kernel(
         def s_items(k):
             items = []
             if 0 <= k - 2 < UNITS:
-                items.append(lambda: interleave(k - 2))
                 items.append(lambda: copy_t(k - 2, 0))
                 items.append(lambda: copy_t(k - 2, 1))
+            if k + 1 < UNITS:
+                items.append(lambda: norms(k + 1))
             if 1 <= k <= 6:
                 for b in range(3):
                     items.append(lambda b=b: w_copy(k - 1, b))
             if k + 1 < UNITS:
                 for lo in range(0, GROUPS, 8):
-                    items.append(lambda lo=lo: squares(k + 1, lo, lo + 8))
-                items.append(lambda: norms(k + 1))
-                if proj_of(k + 1) == 2:
-                    for lo in range(0, GROUPS, 16):
-                        items.append(lambda lo=lo: scale_v(k + 1, lo, lo + 16))
+                    items.append(lambda lo=lo: scale_g(k + 1, lo, lo + 8))
             return items
 
         def v_step(k):
@@ -430,15 +444,15 @@ def tile_torchgemma4visionattention_pa_v_kernel(
                 if quant:
                     quant_f(k - 2)
                 rope_add(k, 0)
-            if prev:
-                dots(k - 1)
+            elif k < UNITS:
+                products(k)
             if 2 <= k <= 7:
                 w_quant(k - 2)
             if rope:
                 rope_add(k, 1)
             if prev:
                 coefs(k - 1)
-            if k < UNITS:
+            if rope:
                 products(k)
             if k in (0, 7):
                 x_inter(k // 7)
@@ -451,18 +465,35 @@ def tile_torchgemma4visionattention_pa_v_kernel(
             if k in (0, 7):
                 x_quant(k // 7)
 
-        squares(0, 0, GROUPS)
+        squares(0)
+        acc = fold(st[0]["gr"])
+        st[0]["ss"] = fold_sum(acc, fold_copy(acc))
         norms(0)
         for k in range(UNITS + 3):
+            tasks = list(mx.get(k, []))
+            waiting = []
+            dot_acc = ss_acc = None
             if 0 <= k - 1 < UNITS:
-                fold(k - 1)
+                dot_acc = fold(st[k - 1]["prod"])
+            if k == 2:
+                rescale(0)
             if 0 <= k - 2 < UNITS:
                 transposes(k - 2)
+            if k + 1 < UNITS:
+                squares(k + 1)
+                ss_acc = fold(st[k + 1]["gr"])
+            if dot_acc is not None:
+                st[k - 1]["dot"] = fold_sum(dot_acc, fold_copy(dot_acc))
+            if tasks:
+                waiting = tasks[0]()
+            if 0 <= k - 2 < UNITS:
+                interleave(k - 2)
+            if ss_acc is not None:
+                st[k + 1]["ss"] = fold_sum(ss_acc, fold_copy(ss_acc))
             if 1 <= k <= 6:
                 w_transposes(k - 1)
             items = s_items(k)
-            tasks = mx.get(k, [])
-            waiting = []
+            tasks = tasks[1:]
             for n in range(max(len(items), len(tasks))):
                 if n < len(items):
                     items[n]()
@@ -474,8 +505,8 @@ def tile_torchgemma4visionattention_pa_v_kernel(
             for copy in waiting:
                 copy()
             v_step(k)
-            if k + 2 < UNITS:
-                load_unit(k + 2)
+            if k + 3 < UNITS:
+                load_unit(k + 3)
             if k + 1 < 6:
                 load_w(k + 1)
             if k == 5:

from contextlib import ExitStack

import concourse.mybir as mybir
from concourse.masks import make_identity

N, D, H, HD = 1024, 768, 16, 64
P = H * HD
PARTS = 128
PACK = 4
PASS = PARTS * PACK
EPS = 1e-6
FLOPS = 2 * 2 * N * D * 3 * P

F32 = mybir.dt.float32
BF16 = mybir.dt.bfloat16
U32 = mybir.dt.uint32
U8 = mybir.dt.uint8
E4 = mybir.dt.float8_e4m3fn_x4
E5 = mybir.dt.float8_e5m2_x4

ALU = mybir.AluOpType
ACT = mybir.ActivationFunctionType
AX = mybir.AxisListType

UNITS = 12
HEADS = 8
GROUPS = PACK * HEADS
FOLDS = 16
QUAD = 4
D_TILES = D // PARTS


def tile_torchgemma4visionattention_pa_v_kernel(
    tc, hidden_states, cos, sin, Wq, Wk, Wv, q_scale, k_scale, yq, yk, yv, grad_0, grad_1, grad_2, out_0, out_1, out_2, out_3
):
    nc = tc.nc
    ys = (yq, yk, yv)
    grads = (grad_0, grad_1, grad_2)
    ws = (Wq, Wk, Wv)
    dws = (out_1, out_2, out_3)

    def proj_of(i):
        return i % 3

    def half_of(i):
        return (i // 3) % 2

    def g_of(i):
        return i // 6

    with ExitStack() as ctx:
        const = ctx.enter_context(tc.tile_pool(name="const", bufs=1))
        io = ctx.enter_context(tc.tile_pool(name="io", bufs=3))
        work = ctx.enter_context(tc.tile_pool(name="work", bufs=2))
        stat = ctx.enter_context(tc.tile_pool(name="stat", bufs=3))
        keep = ctx.enter_context(tc.tile_pool(name="keep", bufs=8))
        stage = ctx.enter_context(tc.tile_pool(name="stage", bufs=4))
        ps_red = ctx.enter_context(tc.psum_pool(name="ps_red", bufs=2))
        ps_tp = ctx.enter_context(tc.psum_pool(name="ps_tp", bufs=2))
        ps_mx = ctx.enter_context(tc.psum_pool(name="ps_mx", bufs=4))

        ident = const.tile([PARTS, PARTS], F32)
        make_identity(nc, ident[:])
        picks = const.tile([PARTS, GROUPS], F32)
        nc.vector.tensor_reduce(out=picks[:], in_=ident[:].rearrange("p (g q) -> p g q", q=QUAD), axis=AX.X, op=ALU.add)
        w_codes = const.tile([PARTS, 6, D], U32, align_bytes=64)
        w_scales = const.tile([PARTS, 6, D], U8, align_bytes=64)
        x_codes = const.tile([PARTS, 2, D], U32, align_bytes=64)
        x_scales = const.tile([PARTS, 2, D], U8, align_bytes=64)

        st = [dict() for i in range(UNITS)]
        raws = dict()

        def load_unit(i):
            rows = slice(g_of(i) * PASS, (g_of(i) + 1) * PASS)
            cols = slice(half_of(i) * PASS, (half_of(i) + 1) * PASS)
            y = io.tile([PARTS, PACK, PASS], F32, bufs=4)
            nc.sync.dma_start(out=y[:], in_=ys[proj_of(i)][rows, cols].rearrange("(p j) w -> p j w", j=PACK))
            g = io.tile([PARTS, PACK, PASS], BF16)
            gsrc = grads[proj_of(i)].rearrange("n h f -> n (h f)")
            nc.sync.dma_start(out=g[:], in_=gsrc[rows, cols].rearrange("(p j) w -> p j w", j=PACK))
            st[i]["y"] = y
            st[i]["g"] = g

        def load_w(c):
            raw = work.tile([PARTS, D_TILES, PASS], BF16, tag="raw", name="w_raw", align_bytes=64)
            cols = slice(half_of(c) * PASS, (half_of(c) + 1) * PASS)
            nc.sync.dma_start(out=raw[:], in_=ws[proj_of(c)][:, cols].rearrange("(t p) w -> p t w", p=PARTS))
            raws["w", c] = raw

        def load_x(g):
            raw = work.tile([PARTS, PACK, D], BF16, tag="raw", name="x_raw", align_bytes=64)
            nc.sync.dma_start(out=raw[:], in_=hidden_states[g * PASS : (g + 1) * PASS, :].rearrange("(p j) w -> p j w", j=PACK))
            raws["x", g] = raw

        c_raw = const.tile([PARTS, 2, PACK, HD], BF16)
        s_raw = const.tile([PARTS, 2, PACK, HD], BF16)
        qs = const.tile([PARTS, HD], BF16)
        ks = const.tile([PARTS, HD], BF16)
        load_unit(0)
        nc.sync.dma_start(out=c_raw[:], in_=cos.rearrange("(g p j) f -> p g j f", g=2, j=PACK))
        nc.sync.dma_start(out=s_raw[:], in_=sin.rearrange("(g p j) f -> p g j f", g=2, j=PACK))
        nc.sync.dma_start(out=qs[:], in_=q_scale.partition_broadcast(PARTS))
        nc.sync.dma_start(out=ks[:], in_=k_scale.partition_broadcast(PARTS))
        load_unit(1)
        load_x(0)
        load_unit(2)
        load_w(0)

        tabs = []
        for scale, tname in ((qs, "tab_q"), (ks, "tab_k")):
            tab = const.tile([PARTS, 2 * PACK, 2, HD], F32, name=tname)
            nc.vector.tensor_tensor(
                out=tab[:, :, 0, :],
                in0=c_raw[:].rearrange("p g j f -> p (g j) f"),
                in1=scale[:].unsqueeze(1).to_broadcast([PARTS, 2 * PACK, HD]),
                op=ALU.mult,
            )
            t6 = tab[:].rearrange("p t s (b k i) -> p t s b k i", b=2, k=2)
            s5 = s_raw[:].rearrange("p g j (b k i) -> p (g j) b k i", b=2, k=2)
            q4 = scale[:].rearrange("p (b k i) -> p b k i", b=2, k=2)
            for k in range(2):
                for b in range(2):
                    nc.vector.tensor_tensor(
                        out=t6[:, :, 1, b, k, :],
                        in0=s5[:, :, b, k, :],
                        in1=q4[:, b, 1 - k, :].unsqueeze(1).to_broadcast([PARTS, 2 * PACK, 16]),
                        op=ALU.mult,
                    )
            tabs.append(tab)

        def folded(tile):
            return tile[:].rearrange("p (b g q) -> p g b q", b=FOLDS, q=QUAD)

        def squares(i):
            gr = io.tile([PARTS, GROUPS * HD], F32, tag="gr", name="gr")
            st[i]["gr"] = gr
            nc.scalar.activation(
                out=folded(gr),
                in_=st[i]["y"][:].rearrange("p j (h b q) -> p (j h) b q", b=FOLDS, q=QUAD),
                func=ACT.Square,
            )

        def fold(src):
            acc = ps_red.tile([PARTS, PASS], F32, tag="red", name="red")
            for b in range(FOLDS):
                nc.tensor.matmul(
                    out=acc[:, 0:PARTS],
                    lhsT=src[:, b * PARTS : (b + 1) * PARTS],
                    rhs=ident[:],
                    start=(b == 0),
                    stop=(b == FOLDS - 1),
                    is_transpose=True,
                )
            return acc

        def fold_copy(acc):
            part = stat.tile([PARTS, PARTS], F32, tag="fold", name="part_sum")
            nc.scalar.copy(out=part[:], in_=acc[:, 0:PARTS])
            return part

        def fold_sum(acc, part):
            res = acc[:, PARTS : PARTS + GROUPS]
            nc.tensor.matmul(out=res, lhsT=part[:], rhs=picks[:], start=True, stop=True)
            return res

        def norms(i):
            r = stat.tile([PARTS, GROUPS], F32)
            nc.scalar.activation(out=r[:], in_=st[i]["ss"], func=ACT.Abs_reciprocal_sqrt, scale=1.0 / HD, bias=EPS)
            rr = stat.tile([PARTS, GROUPS], F32)
            nc.scalar.activation(out=rr[:], in_=r[:], func=ACT.Square)
            st[i]["r"] = r
            st[i]["rr"] = rr

        def scale_g(i, lo, hi):
            for q in range(lo, hi):
                cols = slice(q * HD, (q + 1) * HD)
                nc.scalar.activation(
                    out=st[i]["gr"][:, cols],
                    in_=st[i]["g"][:].rearrange("p j c -> p (j c)")[:, cols],
                    func=ACT.Copy,
                    scale=st[i]["r"][:, q : q + 1],
                )

        def rope_products(i):
            dn = work.tile([PARTS, GROUPS * HD], F32, tag="dn", name="dn")
            gs = work.tile([PARTS, GROUPS * HD], F32, tag="gs", name="gs", bufs=1)
            st[i]["dn"] = dn
            st[i]["gs"] = gs
            tab = tabs[proj_of(i)]
            src = st[i]["g"][:].rearrange("p j c -> p (j c)") if i == 0 else st[i]["gr"][:]
            shape = [PARTS, PACK, HEADS, HD]
            slots = slice(g_of(i) * PACK, (g_of(i) + 1) * PACK)
            for n, dst in ((0, dn), (1, gs)):
                nc.vector.tensor_tensor(
                    out=dst[:].rearrange("p (j h f) -> p j h f", j=PACK, f=HD),
                    in0=src.rearrange("p (j h f) -> p j h f", j=PACK, f=HD),
                    in1=tab[:, slots, n, :].unsqueeze(2).to_broadcast(shape),
                    op=ALU.mult,
                )

        def rope_add(i, k):
            dn = st[i]["dn"][:].rearrange("p (q k i) -> p q k i", k=2, i=16)
            gs = st[i]["gs"][:].rearrange("p (q k i) -> p q k i", k=2, i=16)
            nc.vector.tensor_tensor(
                out=dn[:, :, k, :], in0=dn[:, :, k, :], in1=gs[:, :, 1 - k, :], op=ALU.add if k == 0 else ALU.subtract
            )

        def products(i):
            if proj_of(i) == 2:
                dst = work.tile([PARTS, GROUPS * HD], F32, tag="dn", name="prod_v")
                src = st[i]["gr"]
            else:
                dst, src = st[i]["gr"], st[i]["dn"]
            nc.vector.tensor_tensor(
                out=folded(dst),
                in0=src[:].rearrange("p (g b q) -> p g b q", b=FOLDS, q=QUAD),
                in1=st[i]["y"][:].rearrange("p j (h b q) -> p (j h) b q", b=FOLDS, q=QUAD),
                op=ALU.mult,
            )
            st[i]["prod"] = dst

        def coefs(i):
            nb = stat.tile([PARTS, GROUPS], F32)
            nc.vector.scalar_tensor_tensor(
                out=nb[:], in0=st[i]["dot"], scalar=-1.0 / HD, in1=st[i]["rr"][:], op0=ALU.mult, op1=ALU.mult
            )
            st[i]["nb"] = nb

        def finish(i):
            dy = work.tile([PARTS, PACK, PASS], BF16)
            base = st[i]["gr"] if proj_of(i) == 2 else st[i]["dn"]
            for q in range(GROUPS):
                j, h = q // HEADS, q % HEADS
                cols = slice(h * HD, (h + 1) * HD)
                nc.vector.scalar_tensor_tensor(
                    out=st[i]["gr"][:, q * HD : (q + 1) * HD] if i == 0 else dy[:, j, cols],
                    in0=st[i]["y"][:, j, cols],
                    scalar=st[i]["nb"][:, q : q + 1],
                    in1=base[:, q * HD : (q + 1) * HD],
                    op0=ALU.mult,
                    op1=ALU.add,
                )
            st[i]["dy"] = dy

        def rescale(i):
            for q in range(GROUPS):
                j, h = q // HEADS, q % HEADS
                nc.scalar.activation(
                    out=st[i]["dy"][:, j, h * HD : (h + 1) * HD],
                    in_=st[i]["gr"][:, q * HD : (q + 1) * HD],
                    func=ACT.Copy,
                    scale=st[i]["r"][:, q : q + 1],
                )

        def transposes(i):
            words = st[i]["dy"][:].rearrange("p j c -> p (j c)").bitcast(F32)
            half_words = PASS // 2
            st[i]["tp"] = []
            for b in range(2):
                bank = ps_tp.tile([PARTS, 2, 2, PARTS], F32, tag="tp", name="tp")
                for jj in range(2):
                    j = 2 * b + jj
                    for u in range(2):
                        nc.tensor.transpose(bank[:, jj, u, :], words[:, j * half_words + u : (j + 1) * half_words : 2], ident[:])
                st[i]["tp"].append(bank)

        def copy_t(i, b):
            if b == 0:
                dyt = work.tile([PARTS, PASS, PACK], BF16, align_bytes=64)
                st[i]["dyt"] = dyt
            words = st[i]["dyt"][:].rearrange("p n t -> p (n t)").bitcast(F32)
            dst = words[:, b * PASS : (b + 1) * PASS].rearrange("p (j n u) -> p j n u", j=2, u=2)
            nc.scalar.copy(out=dst, in_=st[i]["tp"][b][:].rearrange("p j u n -> p j n u"))

        def interleave(i):
            dyi = work.tile([PARTS, PASS, PACK], BF16, align_bytes=64)
            nc.scalar.copy(
                out=dyi[:].rearrange("p (c i) j -> p c j i", i=4),
                in_=st[i]["dy"][:].rearrange("p j (c i) -> p c j i", i=4),
            )
            st[i]["dyi"] = dyi

        def quant_f(i):
            fc = keep.tile([PARTS, PASS], U32, align_bytes=64)
            fs = keep.tile([PARTS, PASS], U8, align_bytes=64)
            nc.vector.quantize_mx(out=fc[:].bitcast(E5), scales=fs[:], in_=st[i]["dyt"][:].rearrange("p n t -> p (n t)"))
            st[i]["f"] = (fc, fs)

        def quant_t(i):
            tcod = keep.tile([PARTS, PASS], U32, align_bytes=64)
            tsc = keep.tile([PARTS, PASS], U8, align_bytes=64)
            nc.vector.quantize_mx(out=tcod[:].bitcast(E5), scales=tsc[:], in_=st[i]["dyi"][:].rearrange("p c j -> p (c j)"))
            st[i]["t"] = (tcod, tsc)

        def quant_768(src, codes, scales):
            flat = src[:].rearrange("p n t -> p (n t)")
            for lo, hi in ((0, 512), (512, 768)):
                nc.vector.quantize_mx(
                    out=codes[:, lo:hi].bitcast(E4), scales=scales[:, lo:hi], in_=flat[:, lo * PACK : hi * PACK]
                )

        def w_transposes(c):
            raws["wt", c] = []
            words = raws["w", c][:].rearrange("p t w -> p (t w)").bitcast(F32)
            half_words = PASS // 2
            for b in range(3):
                bank = ps_tp.tile([PARTS, 2, 2, PARTS], F32, tag="tp", name="tp")
                for tt in range(2):
                    t = 2 * b + tt
                    for u in range(2):
                        nc.tensor.transpose(bank[:, tt, u, :], words[:, t * half_words + u : (t + 1) * half_words : 2], ident[:])
                raws["wt", c].append(bank)

        def w_copy(c, b):
            if b == 0:
                grp = work.tile([PARTS, D, PACK], BF16, tag="grp", name="w_grp", align_bytes=64, bufs=1)
                raws["wg", c] = grp
            words = raws["wg", c][:].rearrange("p n t -> p (n t)").bitcast(F32)
            dst = words[:, b * PASS : (b + 1) * PASS].rearrange("p (j n u) -> p j n u", j=2, u=2)
            nc.scalar.copy(out=dst, in_=raws["wt", c][b][:].rearrange("p j u n -> p j n u"))

        def w_quant(c):
            quant_768(raws["wg", c], w_codes[:, c, :], w_scales[:, c, :])

        def x_inter(g):
            grp = work.tile([PARTS, D, PACK], BF16, tag="grp", name="x_grp", align_bytes=64, bufs=1)
            nc.vector.tensor_copy(out=grp[:], in_=raws["x", g][:].rearrange("p j w -> p w j"))
            raws["xg", g] = grp

        def x_quant(g):
            quant_768(raws["xg", g], x_codes[:, g, :], x_scales[:, g, :])

        def copy_out(engine, out, in_):
            if engine == "s":
                nc.scalar.copy(out=out, in_=in_)
            else:
                nc.vector.tensor_copy(out=out, in_=in_)

        def dw_task(i, t, engine):
            acc = ps_mx.tile([PARTS, PASS], F32, tag="mx", name="acc")
            for g in range(2):
                src = i - 6 + 6 * g
                tcod, tsc = st[src]["t"]
                lanes = slice(t * PARTS, (t + 1) * PARTS)
                nc.tensor.matmul_mx(
                    out=acc[:],
                    lhsT=x_codes[:, g, lanes].bitcast(E4),
                    lhsT_scale=x_scales[:, g, lanes],
                    rhs=tcod[:].bitcast(E5),
                    rhs_scale=tsc[:],
                    start=(g == 0),
                    stop=(g == 1),
                )

            def empty():
                res = stage.tile([PARTS, PASS], F32, tag="dw", name="res")
                copy_out(engine, res[:], acc[:])
                cols = slice(half_of(i) * PASS, (half_of(i) + 1) * PASS)
                nc.sync.dma_start(out=dws[proj_of(i)][t * PARTS : (t + 1) * PARTS, cols], in_=res[:])

            return [empty]

        def dx_task(g, j, units, engine, mode):
            banks = []
            for d0 in (0, D - PASS):
                acc = ps_mx.tile([PARTS, PASS], F32, tag="mx", name="acc")
                banks.append(acc)
            lanes = slice(j * PARTS, (j + 1) * PARTS)
            for n, i in enumerate(units):
                fc, fs = st[i]["f"]
                for acc, d0 in zip(banks, (0, D - PASS)):
                    nc.tensor.matmul_mx(
                        out=acc[:],
                        lhsT=fc[:, lanes].bitcast(E5),
                        lhsT_scale=fs[:, lanes],
                        rhs=w_codes[:, i % 6, d0 : d0 + PASS].bitcast(E4),
                        rhs_scale=w_scales[:, i % 6, d0 : d0 + PASS],
                        start=(n == 0),
                        stop=(n == len(units) - 1),
                    )
            rest = D - PASS

            def store(res):
                dst = out_0[g * PASS : (g + 1) * PASS, :].rearrange("(p j) d -> p j d", j=PACK)
                nc.sync.dma_start(out=dst[:, j, :], in_=res)

            def empty():
                if mode == "part":
                    if j % 2 == 0:
                        part = work.tile([PARTS, 2, D], F32, tag="raw", name="part", align_bytes=64)
                        raws["part", j // 2] = part
                    res = raws["part", j // 2][:, j % 2, :]
                else:
                    full = stage.tile([PARTS, D], F32, tag="dx", name="full", bufs=2)
                    res = full[:]
                pieces = ((slice(0, PASS), banks[0][:]), (slice(PASS, D), banks[1][:, PASS - rest :]))
                for cols, src in pieces:
                    if mode == "add":
                        nc.vector.tensor_tensor(out=res[:, cols], in0=src, in1=raws["part", j // 2][:, j % 2, cols], op=ALU.add)
                    else:
                        copy_out(engine, res[:, cols], src)
                if mode != "part":
                    store(res)

            return [empty]

        mx = dict()
        mx[8] = [lambda j=j: dx_task(0, j, range(6), "s", "full") for j in (0, 1)]
        mx[9] = [lambda: dx_task(0, 2, range(6), "s", "full")] + [lambda t=t: dw_task(6, t, "s") for t in range(D_TILES)]
        mx[10] = [lambda: dx_task(0, 3, range(6), "s", "full")] + [lambda t=t: dw_task(7, t, "s") for t in range(D_TILES)]
        mx[11] = [lambda t=t: dw_task(8, t, "s") for t in range(D_TILES)] + [
            lambda j=j: dx_task(1, j, range(6, 9), "s", "part") for j in (0, 1)
        ]
        mx[12] = [lambda t=t: dw_task(9, t, "s") for t in range(D_TILES)] + [
            lambda j=j: dx_task(1, j, range(6, 9), "s", "part") for j in (2, 3)
        ]
        mx[13] = [lambda t=t: dw_task(10, t, "s") for t in range(D_TILES)]
        mx[14] = [lambda j=j: dx_task(1, j, range(9, 12), "v", "add") for j in range(4)] + [
            lambda t=t: dw_task(11, t, "s") for t in range(D_TILES)
        ]

        def s_items(k):
            items = []
            if 0 <= k - 2 < UNITS:
                items.append(lambda: copy_t(k - 2, 0))
                items.append(lambda: copy_t(k - 2, 1))
            if k + 1 < UNITS:
                items.append(lambda: norms(k + 1))
            if 1 <= k <= 6:
                for b in range(3):
                    items.append(lambda b=b: w_copy(k - 1, b))
            if k + 1 < UNITS:
                for lo in range(0, GROUPS, 8):
                    items.append(lambda lo=lo: scale_g(k + 1, lo, lo + 8))
            return items

        def v_step(k):
            rope = k < UNITS and proj_of(k) < 2
            prev = 0 <= k - 1 < UNITS
            quant = 0 <= k - 2 < UNITS
            if rope:
                rope_products(k)
                if quant:
                    quant_f(k - 2)
                rope_add(k, 0)
            elif k < UNITS:
                products(k)
            if 2 <= k <= 7:
                w_quant(k - 2)
            if rope:
                rope_add(k, 1)
            if prev:
                coefs(k - 1)
            if rope:
                products(k)
            if k in (0, 7):
                x_inter(k // 7)
            if prev:
                finish(k - 1)
            if quant and not rope:
                quant_f(k - 2)
            if quant:
                quant_t(k - 2)
            if k in (0, 7):
                x_quant(k // 7)

        squares(0)
        acc = fold(st[0]["gr"])
        st[0]["ss"] = fold_sum(acc, fold_copy(acc))
        norms(0)
        for k in range(UNITS + 3):
            tasks = list(mx.get(k, []))
            waiting = []
            dot_acc = ss_acc = None
            if 0 <= k - 1 < UNITS:
                dot_acc = fold(st[k - 1]["prod"])
            if k == 2:
                rescale(0)
            if 0 <= k - 2 < UNITS:
                transposes(k - 2)
            if k + 1 < UNITS:
                squares(k + 1)
                ss_acc = fold(st[k + 1]["gr"])
            if dot_acc is not None:
                st[k - 1]["dot"] = fold_sum(dot_acc, fold_copy(dot_acc))
            if tasks:
                waiting = tasks[0]()
            if 0 <= k - 2 < UNITS:
                interleave(k - 2)
            if ss_acc is not None:
                st[k + 1]["ss"] = fold_sum(ss_acc, fold_copy(ss_acc))
            if 1 <= k <= 6:
                w_transposes(k - 1)
            items = s_items(k)
            tasks = tasks[1:]
            for n in range(max(len(items), len(tasks))):
                if n < len(items):
                    items[n]()
                for copy in waiting:
                    copy()
                waiting = []
                if n < len(tasks):
                    waiting = tasks[n]()
            for copy in waiting:
                copy()
            v_step(k)
            if k + 3 < UNITS:
                load_unit(k + 3)
            if k + 1 < 6:
                load_w(k + 1)
            if k == 5:
                load_x(1)
